import numpy as np
import ml_dtypes


def mxq(x, axis, fmt="e4m3"):
    dtype, down = {"e4m3": (ml_dtypes.float8_e4m3fn, 7), "e5m2": (ml_dtypes.float8_e5m2, 14)}[fmt]
    v = np.moveaxis(np.asarray(x, np.float32).astype(ml_dtypes.bfloat16).astype(np.float64), axis, -1)
    blocks = v.reshape(v.shape[:-1] + (-1, 32))
    amax = np.abs(blocks).max(-1, keepdims=True)
    byte = np.maximum(np.where(amax > 0, np.frexp(amax)[1] - 1 + 127, 0) - down, 1)
    scale = np.exp2(byte - 127.0)
    codes = (blocks / scale).astype(np.float32).astype(dtype).astype(np.float64)
    return np.moveaxis((codes * scale).reshape(v.shape), -1, axis)


WIDE = False


def mx_kscale(k):
    if not WIDE:
        return np.ones(k)
    levels = np.array([10, -10, 5, -5, 0])
    a = np.random.permutation(np.resize(levels, k // 512 * 4)).reshape(k // 512, 4)
    idx = np.arange(k)
    return np.exp2(a[idx // 512, idx % 128 // 32])


BF16 = ml_dtypes.bfloat16


def bf(x):
    return np.asarray(x, np.float32).astype(BF16)


def f64(x):
    return np.asarray(x).astype(np.float64)


E2M1 = np.array([0.0, 0.5, 1.0, 1.5, 2.0, 3.0, 4.0, 6.0, -0.0, -0.5, -1.0, -1.5, -2.0, -3.0, -4.0, -6.0])


def pack_weight(w, fmt):
    k, n = w.shape
    w = f64(bf(w)).reshape(k // 32, 32, n)
    amax = np.abs(w).max(1)
    if fmt == "e4m3":
        byte = np.frexp(amax)[1] - 1 + 127 - 7
    else:
        mant, ex = np.frexp(amax / 6.0)
        byte = np.where(mant > 0.5, ex, ex - 1) + 127
    byte = np.clip(np.where(amax > 0, byte, 1), 1, 254)
    scaled = (w * np.exp2(127.0 - byte)[:, None, :]).reshape(k, n).astype(np.float32)
    by_word = np.ascontiguousarray(scaled.reshape(k // 512, 128, 4, n).transpose(0, 1, 3, 2))
    if fmt == "e4m3":
        words = by_word.astype(ml_dtypes.float8_e4m3fn).view(np.uint8)
    else:
        c = by_word.astype(ml_dtypes.float4_e2m1fn).view(np.uint8) & 0xF
        words = c[..., 0::2] | (c[..., 1::2] << 4)
    return np.ascontiguousarray(words), np.ascontiguousarray(byte.astype(np.uint8).reshape(k // 512, 16, n))


def unpack_weight(words, scales, fmt):
    g, p, n, _ = words.shape
    if fmt == "e4m3":
        vals = np.ascontiguousarray(words).view(ml_dtypes.float8_e4m3fn).astype(np.float64)
    else:
        nib = np.empty((g, p, n, 4), np.uint8)
        nib[..., 0::2] = words & 0xF
        nib[..., 1::2] = words >> 4
        vals = E2M1[nib]
    vals = vals * np.repeat(np.exp2(scales.astype(np.float64) - 127.0), 8, axis=1)[..., None]
    return vals.transpose(0, 1, 3, 2).reshape(g * 512, n)


B, I, H = 128, 1024, 2048
K = I + H
DT = 1.0
EPS = 1e-6
FMT = "e4m3"


def softplus(v):
    return np.logaddexp(v, 0.0)


def sigmoid(v):
    return 1.0 / (1.0 + np.exp(-v))


def setup_inputs():
    s = np.concatenate([mx_kscale(K)[:I], np.ones(H)])
    scale = (6.0 / ((1 + 5.0) * K)) ** 0.5
    x = bf(np.random.standard_normal((B, I)) * s[:I])
    hidden = bf(np.random.standard_normal((B, H)))
    W_tau_words, W_tau_scales = pack_weight((np.random.uniform(-scale, scale, (H, K)) / s).T, FMT)
    b_tau = bf(np.random.standard_normal(H) * 0.1)
    W_r_words, W_r_scales = pack_weight((np.random.uniform(-scale, scale, (H, K)) / s).T, FMT)
    b_r = bf(np.random.standard_normal(H) * 0.1)
    W_h_words, W_h_scales = pack_weight((np.random.uniform(-scale, scale, (H, K)) / s).T, FMT)
    b_h = bf(np.random.standard_normal(H) * 0.1)
    return {"x": x,
            "hidden": hidden,
            "W_tau_words": W_tau_words,
            "W_tau_scales": W_tau_scales,
            "b_tau": b_tau,
            "W_r_words": W_r_words,
            "W_r_scales": W_r_scales,
            "b_r": b_r,
            "W_h_words": W_h_words,
            "W_h_scales": W_h_scales,
            "b_h": b_h}


def reference(x, hidden, W_tau_words, W_tau_scales, b_tau, W_r_words, W_r_scales, b_r, W_h_words, W_h_scales, b_h):
    x, hidden = f64(x), f64(hidden)
    combined = np.concatenate([x, hidden], axis=1)
    cq = mxq(combined, 1, "e4m3")
    tau = softplus((cq @ unpack_weight(W_tau_words, W_tau_scales, FMT)) + f64(b_tau)) + EPS
    r = sigmoid((cq @ unpack_weight(W_r_words, W_r_scales, FMT)) + f64(b_r))
    gated = r * hidden
    cand_in = np.concatenate([x, gated], axis=1)
    h_tilde = np.tanh((mxq(cand_in, 1, "e4m3") @ unpack_weight(W_h_words, W_h_scales, FMT)) + f64(b_h))
    return hidden + DT * (h_tilde - hidden) / tau

@@ -1,0 +1,319 @@
+from contextlib import ExitStack
+
+import concourse.mybir as mybir
+from concourse.masks import make_identity
+
+F32 = mybir.dt.float32
+BF16 = mybir.dt.bfloat16
+I32 = mybir.dt.int32
+U32 = mybir.dt.uint32
+U8 = mybir.dt.uint8
+FP8X4 = mybir.dt.float8_e4m3fn_x4
+ALU = mybir.AluOpType
+ACT = mybir.ActivationFunctionType
+
+P = 128
+I_DIM = 1024
+H_DIM = 2048
+GROUPS = 6
+NT = 512
+CHUNKS = H_DIM // NT
+EPS = 1e-6
+
+FLOPS = 3 * 2 * 128 * 3072 * 2048
+
+
+def tile_ltccell_w_kernel(
+    tc, x, hidden, wt_words, wt_scales, b_tau, wr_words, wr_scales, b_r, wh_words, wh_scales, b_h, out
+):
+    nc = tc.nc
+    with ExitStack() as ctx:
+        ctx.enter_context(tc.manual_schedule())
+        const = ctx.enter_context(tc.tile_pool(name="const", bufs=1))
+        wpool = ctx.enter_context(tc.tile_pool(name="wpool", bufs=13))
+        psum = ctx.enter_context(tc.psum_pool(name="psum", bufs=1))
+        cols = [slice(NT * c, NT * (c + 1)) for c in range(CHUNKS)]
+
+        planes = {}
+        for nm in ("t", "r", "h"):
+            planes[nm] = const.tile([P, 2, H_DIM], U8, align_bytes=64, name="planes_" + nm)
+        brow = const.tile([P, H_DIM], BF16, name="brow")
+        one_col = const.tile([P, 1], F32, name="one_col")
+        eps_col = const.tile([P, 1], F32, name="eps_col")
+        nc.vector.memset(planes["t"][:].bitcast(I32), 0)
+        nc.vector.memset(brow[:].bitcast(I32), 0)
+        nc.vector.memset(planes["r"][:].bitcast(I32), 0)
+        nc.vector.memset(planes["h"][:].bitcast(I32), 0)
+        nc.vector.memset(one_col[:], 1.0)
+        nc.vector.memset(eps_col[:], EPS)
+        identf = const.tile([P, P], F32, name="identf")
+        identb = const.tile([P, P], BF16, name="identb")
+        make_identity(nc, identf[:])
+        make_identity(nc, identb[:])
+
+        def load_words(words, g0, g1, n0, n1, name):
+            t = wpool.tile([P, g1 - g0, n1 - n0], U32, tag="w", name=name, align_bytes=64)
+            src = words[g0:g1, :, n0:n1, :].rearrange("g p n t -> p g (n t)").bitcast(I32)
+            nc.sync.dma_start(out=t[:].bitcast(I32), in_=src)
+            return t
+
+        def load_scales(nm, scales, blk, q):
+            ng = 4 if blk == 0 else 2
+            nc.sync.dma_start(
+                out=planes[nm][32 * q : 32 * q + 4 * ng, blk, :].bitcast(I32),
+                in_=scales[4 * blk : 4 * blk + ng, 4 * q : 4 * q + 4, :].bitcast(I32),
+            )
+
+        def load_half_piece(table, words, i, name):
+            half = i // 3
+            g0 = 2 * (i % 3)
+            t = load_words(words, g0, g0 + 2, 2 * NT * half, 2 * NT * (half + 1), "%s%d" % (name, i))
+            for g in (g0, g0 + 1):
+                for cc in range(2):
+                    table[(g, 2 * half + cc)] = t[:, g - g0, NT * cc : NT * (cc + 1)]
+
+        x_sb = const.tile([P, I_DIM], BF16, name="x_sb")
+        hid_sb = const.tile([P, H_DIM], BF16, name="hid_sb")
+        nc.sync.dma_start(out=x_sb[:], in_=x)
+        nc.sync.dma_start(out=hid_sb[:], in_=hidden)
+        for j, b in enumerate((b_tau, b_r, b_h)):
+            nc.scalar.dma_start(out=brow[j : j + 1, :], in_=b.unsqueeze(0))
+
+        wt = {}
+        wr = {}
+        wh = {}
+        later = [(blk, q) for blk in range(2) for q in range(4)]
+        load_half_piece(wt, wt_words, 0, "wt")
+        for q in range(4):
+            load_scales("t", wt_scales, 0, q)
+        load_half_piece(wt, wt_words, 1, "wt")
+        for q in range(4):
+            load_scales("t", wt_scales, 1, q)
+        for i in range(2, 6):
+            load_half_piece(wt, wt_words, i, "wt")
+            for blk, q in later[2 * (i - 2) : 2 * (i - 1)]:
+                load_scales("r", wr_scales, blk, q)
+        for i in range(6):
+            load_half_piece(wr, wr_words, i, "wr")
+            if i < 4:
+                for blk, q in later[2 * i : 2 * (i + 1)]:
+                    load_scales("h", wh_scales, blk, q)
+
+        codes = const.tile([P, GROUPS * P], U32, align_bytes=64, name="codes")
+        ascl = const.tile([P, GROUPS * P], U8, align_bytes=64, name="ascl")
+        xw = x_sb[:].bitcast(F32)
+        hw = hid_sb[:].bitcast(F32)
+        tps = []
+        for j in range(3):
+            tp = psum.tile([P, 4, P], F32, tag="p%d" % (4 + j), name="tp%d" % j)
+            for gi in range(2):
+                g = 2 * j + gi
+                srcw = xw if g < 2 else hw
+                base = 256 * g if g < 2 else 256 * (g - 2)
+                for u in range(2):
+                    nc.tensor.transpose(tp[:, 2 * gi + u, :], srcw[:, base + u : base + 256 : 2], identf[:])
+            tps.append(tp)
+        grouped = [const.tile([P, 2 * NT], BF16, align_bytes=64, name="grp%d" % j) for j in range(3)]
+        for j in (0, 1, 2):
+            dst = grouped[j][:].bitcast(F32).rearrange("p (g b u) -> p g b u", g=2, u=2)
+            src = tps[j][:].rearrange("p (g u) b -> p g b u", g=2)
+            if j == 1:
+                nc.scalar.copy(out=dst, in_=src)
+            else:
+                nc.vector.tensor_copy(out=dst, in_=src)
+        for j in range(3):
+            nc.vector.quantize_mx(
+                out=codes[:, 256 * j : 256 * (j + 1)].bitcast(FP8X4),
+                scales=ascl[:, 256 * j : 256 * (j + 1)],
+                in_=grouped[j][:],
+            )
+        hh = const.tile([P, H_DIM], BF16, name="hh")
+        nc.vector.tensor_scalar_mul(out=hh[:], in0=hid_sb[:], scalar1=0.5)
+
+        bbc = []
+        tags = [7, 4, 5, 6, 7, 4]
+        for j in range(3):
+            bb = const.tile([P, H_DIM], BF16, name="bbc%d" % j)
+            for half in range(2):
+                pb = psum.tile([P, 2 * NT], BF16, tag="p%d" % tags[2 * j + half], name="pb%d_%d" % (j, half))
+                for s in range(2):
+                    lo = 2 * NT * half + NT * s
+                    nc.tensor.matmul(
+                        out=pb[:, NT * s : NT * (s + 1)],
+                        lhsT=identb[:, j : j + 1].to_broadcast([P, P]),
+                        rhs=brow[:, lo : lo + NT],
+                        start=True,
+                        stop=True,
+                    )
+                nc.scalar.copy(out=bb[:, 2 * NT * half : 2 * NT * (half + 1)], in_=pb[:])
+            bbc.append(bb)
+
+        def mx_pass(acc, a_codes, a_scl, ga, w_ap, nm, g, c, start, stop):
+            k = 4 * (g % 4)
+            nc.tensor.matmul_mx(
+                out=acc[:],
+                lhsT=a_codes[:, P * ga : P * (ga + 1)].bitcast(FP8X4),
+                lhsT_scale=a_scl[:, P * ga : P * (ga + 1)],
+                rhs=w_ap.bitcast(FP8X4),
+                rhs_scale=planes[nm][k:P, g // 4, NT * c : NT * (c + 1)],
+                start=start,
+                stop=stop,
+            )
+
+        def half_passes(acc, table, nm, half):
+            for g in range(GROUPS):
+                for c in (2 * half, 2 * half + 1):
+                    mx_pass(acc[c], codes, ascl, g, table[(g, c)], nm, g, c, g == 0, g == GROUPS - 1)
+
+        acc_t = [psum.tile([P, NT], F32, tag="p%d" % c, name="acc_t%d" % c) for c in range(CHUNKS)]
+        half_passes(acc_t, wt, "t", 0)
+        half_passes(acc_t, wt, "t", 1)
+
+        for g in range(2):
+            t = load_words(wh_words, g, g + 1, 0, H_DIM, "wh%d" % g)
+            for c in range(CHUNKS):
+                wh[(g, c)] = t[:, 0, cols[c]]
+        for c in range(CHUNKS):
+            pieces = [(2, 6)] if c < CHUNKS - 1 else [(2, 5), (5, 6)]
+            for g0, g1 in pieces:
+                t = load_words(wh_words, g0, g1, NT * c, NT * (c + 1), "wh_%d_%d" % (c, g0))
+                for g in range(g0, g1):
+                    wh[(g, c)] = t[:, g - g0, :]
+
+        v = [const.tile([P, NT], F32, name="v%d" % c) for c in range(CHUNKS)]
+        t1 = [const.tile([P, NT], F32, name="t1_%d" % c) for c in range(CHUNKS)]
+
+        def tau_in(cs):
+            for c in cs:
+                nc.vector.tensor_tensor(out=v[c][:], in0=acc_t[c][:], in1=bbc[0][:, cols[c]], op=ALU.add)
+                nc.vector.scalar_tensor_tensor(
+                    out=t1[c][:], in0=v[c][:], scalar=-1.0, in1=v[c][:], op0=ALU.mult, op1=ALU.min
+                )
+
+        def tau_exp(cs):
+            for c in cs:
+                nc.scalar.activation(out=t1[c][:], in_=t1[c][:], func=ACT.Exp)
+
+        def tau_ln(cs):
+            for c in cs:
+                nc.scalar.activation(out=t1[c][:], in_=t1[c][:], func=ACT.Ln, bias=one_col[:])
+
+        def tau_sum(cs):
+            for c in cs:
+                nc.vector.scalar_tensor_tensor(
+                    out=v[c][:], in0=v[c][:], scalar=0.0, in1=t1[c][:], op0=ALU.max, op1=ALU.add
+                )
+
+        def tau_ln2(cs):
+            for c in cs:
+                nc.scalar.activation(out=t1[c][:], in_=v[c][:], func=ACT.Ln, bias=eps_col[:])
+
+        def tau_recip(cs):
+            for c in cs:
+                nc.scalar.activation(out=v[c][:], in_=t1[c][:], func=ACT.Exp, scale=-1.0)
+
+        def tau_keep(cs):
+            for c in cs:
+                nc.gpsimd.tensor_tensor(out=t1[c][:], in0=hid_sb[:, cols[c]], in1=v[c][:], op=ALU.mult)
+                nc.gpsimd.tensor_tensor(out=t1[c][:], in0=hid_sb[:, cols[c]], in1=t1[c][:], op=ALU.subtract)
+
+        rt = v
+        keep = t1
+        first = (0, 1)
+        second = (2, 3)
+        tau_in(first)
+        tau_exp(first)
+        tau_ln(first)
+        tau_sum(first)
+        tau_ln2(first)
+        tau_recip(first)
+        tau_keep(first)
+        tau_in(second)
+        tau_exp(second)
+        tau_ln(second)
+
+        acc_r = [psum.tile([P, NT], F32, tag="p%d" % (4 + c), name="acc_r%d" % c) for c in range(CHUNKS)]
+        half_passes(acc_r, wr, "r", 0)
+        half_passes(acc_r, wr, "r", 1)
+
+        vr = [const.tile([P, NT], F32, name="vr%d" % c) for c in range(CHUNKS)]
+        gated = [const.tile([P, NT], BF16, name="gated%d" % c) for c in range(CHUNKS)]
+        gg = [const.tile([P, NT], BF16, align_bytes=64, name="gg%d" % c) for c in range(CHUNKS)]
+        gcodes = const.tile([P, CHUNKS * P], U32, align_bytes=64, name="gcodes")
+        gscl = const.tile([P, CHUNKS * P], U8, align_bytes=64, name="gscl")
+        tpg = {}
+
+        def r_in(cs):
+            for c in cs:
+                nc.vector.tensor_tensor(out=vr[c][:], in0=acc_r[c][:], in1=bbc[1][:, cols[c]], op=ALU.add)
+
+        def r_tanh(cs):
+            for c in cs:
+                nc.scalar.activation(out=vr[c][:], in_=vr[c][:], func=ACT.Tanh, scale=0.5)
+
+        def r_gate(cs):
+            for c in cs:
+                nc.vector.scalar_tensor_tensor(
+                    out=gated[c][:], in0=vr[c][:], scalar=1.0, in1=hh[:, cols[c]], op0=ALU.add, op1=ALU.mult
+                )
+
+        def r_transpose(cs):
+            for c in cs:
+                tpg[c] = psum.tile([P, 4, P], BF16, tag="p%d" % (4 + c), name="tpg%d" % c)
+                for t in range(4):
+                    nc.tensor.transpose(tpg[c][:, t, :], gated[c][:, t:NT:4], identb[:])
+
+        def r_copy(cs):
+            for c in cs:
+                nc.scalar.copy(
+                    out=gg[c][:].rearrange("p (b t) -> p b t", t=4), in_=tpg[c][:].rearrange("p t b -> p b t")
+                )
+
+        def r_quant(cs):
+            for c in cs:
+                nc.vector.quantize_mx(
+                    out=gcodes[:, P * c : P * (c + 1)].bitcast(FP8X4),
+                    scales=gscl[:, P * c : P * (c + 1)],
+                    in_=gg[c][:],
+                )
+
+        r_in(first)
+        tau_sum(second)
+        tau_ln2(second)
+        r_tanh(first)
+        tau_recip(second)
+        tau_keep(second)
+        r_gate(first)
+        r_transpose(first)
+        r_in(second)
+        r_copy(first)
+        r_quant(first)
+        r_tanh(second)
+        r_gate(second)
+        acc_h = [psum.tile([P, NT], F32, tag="p%d" % c, name="acc_h%d" % c) for c in range(CHUNKS)]
+        for c in range(CHUNKS):
+            mx_pass(acc_h[c], codes, ascl, 0, wh[(0, c)], "h", 0, c, True, False)
+        r_transpose(second)
+        r_copy(second)
+        r_quant(second)
+        for c in range(CHUNKS):
+            mx_pass(acc_h[c], codes, ascl, 1, wh[(1, c)], "h", 1, c, False, False)
+
+        HALF = NT // 2
+        for c in range(CHUNKS):
+            for g in range(2, GROUPS):
+                mx_pass(acc_h[c], gcodes, gscl, g - 2, wh[(g, c)], "h", g, c, False, g == GROUPS - 1)
+            hz = const.tile([P, NT], F32, name="hz%d" % c)
+            parts = [slice(0, HALF), slice(HALF, NT)]
+            for i, s in enumerate(parts):
+                lo = NT * c + HALF * i
+                nc.vector.tensor_tensor(out=hz[:, s], in0=acc_h[c][:, s], in1=bbc[2][:, lo : lo + HALF], op=ALU.add)
+            for s in parts:
+                nc.scalar.activation(out=hz[:, s], in_=hz[:, s], func=ACT.Tanh)
+            for s in parts:
+                nc.vector.tensor_tensor(out=hz[:, s], in0=hz[:, s], in1=rt[c][:, s], op=ALU.mult)
+                nc.vector.tensor_tensor(out=hz[:, s], in0=hz[:, s], in1=keep[c][:, s], op=ALU.add)
+            if c < CHUNKS - 1:
+                nc.gpsimd.dma_start(out=out[:, cols[c]], in_=hz[:])
+            else:
+                nc.sync.dma_start(out=out[:, cols[c]], in_=hz[:])

@@ -49,7 +49,6 @@ def tile_ltccell_w_kernel(
         identf = const.tile([P, P], F32, name="identf")
         identb = const.tile([P, P], BF16, name="identb")
         make_identity(nc, identf[:])
-        make_identity(nc, identb[:])
 
         def load_words(words, g0, g1, n0, n1, name):
             t = wpool.tile([P, g1 - g0, n1 - n0], U32, tag="w", name=name, align_bytes=64)
@@ -59,9 +58,9 @@ def tile_ltccell_w_kernel(
 
         def load_scales(nm, scales, blk, q):
             ng = 4 if blk == 0 else 2
-            nc.sync.dma_start(
-                out=planes[nm][32 * q : 32 * q + 4 * ng, blk, :].bitcast(I32),
-                in_=scales[4 * blk : 4 * blk + ng, 4 * q : 4 * q + 4, :].bitcast(I32),
+            nc.gpsimd.dma_start(
+                out=planes[nm][32 * q : 32 * q + 4 * ng, blk, :].bitcast(F32),
+                in_=scales[4 * blk : 4 * blk + ng, 4 * q : 4 * q + 4, :].bitcast(F32),
             )
 
         def load_half_piece(table, words, i, name):
@@ -83,21 +82,17 @@ def tile_ltccell_w_kernel(
         wr = {}
         wh = {}
         later = [(blk, q) for blk in range(2) for q in range(4)]
-        load_half_piece(wt, wt_words, 0, "wt")
-        for q in range(4):
-            load_scales("t", wt_scales, 0, q)
-        load_half_piece(wt, wt_words, 1, "wt")
-        for q in range(4):
-            load_scales("t", wt_scales, 1, q)
-        for i in range(2, 6):
+        for blk, q in later:
+            load_scales("t", wt_scales, blk, q)
+        make_identity(nc, identb[:])
+        for blk, q in later:
+            load_scales("r", wr_scales, blk, q)
+        for blk, q in later:
+            load_scales("h", wh_scales, blk, q)
+        for i in range(6):
             load_half_piece(wt, wt_words, i, "wt")
-            for blk, q in later[2 * (i - 2) : 2 * (i - 1)]:
-                load_scales("r", wr_scales, blk, q)
         for i in range(6):
             load_half_piece(wr, wr_words, i, "wr")
-            if i < 4:
-                for blk, q in later[2 * i : 2 * (i + 1)]:
-                    load_scales("h", wh_scales, blk, q)
 
         codes = const.tile([P, GROUPS * P], U32, align_bytes=64, name="codes")
         ascl = const.tile([P, GROUPS * P], U8, align_bytes=64, name="ascl")
@@ -313,7 +308,4 @@ def tile_ltccell_w_kernel(
             for s in parts:
                 nc.vector.tensor_tensor(out=hz[:, s], in0=hz[:, s], in1=rt[c][:, s], op=ALU.mult)
                 nc.vector.tensor_tensor(out=hz[:, s], in0=hz[:, s], in1=keep[c][:, s], op=ALU.add)
-            if c < CHUNKS - 1:
-                nc.gpsimd.dma_start(out=out[:, cols[c]], in_=hz[:])
-            else:
-                nc.sync.dma_start(out=out[:, cols[c]], in_=hz[:])
+            nc.sync.dma_start(out=out[:, cols[c]], in_=hz[:])

@@ -89,8 +89,10 @@ def tile_ltccell_w_kernel(
             load_scales("r", wr_scales, blk, q)
         for blk, q in later:
             load_scales("h", wh_scales, blk, q)
-        for i in range(6):
-            load_half_piece(wt, wt_words, i, "wt")
+        for g in range(GROUPS):
+            t = load_words(wt_words, g, g + 1, 0, H_DIM, "wt%d" % g)
+            for c in range(CHUNKS):
+                wt[(g, c)] = t[:, 0, cols[c]]
         for i in range(6):
             load_half_piece(wr, wr_words, i, "wr")
 
@@ -161,8 +163,9 @@ def tile_ltccell_w_kernel(
                     mx_pass(acc[c], codes, ascl, g, table[(g, c)], nm, g, c, g == 0, g == GROUPS - 1)
 
         acc_t = [psum.tile([P, NT], F32, tag="p%d" % c, name="acc_t%d" % c) for c in range(CHUNKS)]
-        half_passes(acc_t, wt, "t", 0)
-        half_passes(acc_t, wt, "t", 1)
+        for g in range(GROUPS):
+            for c in range(CHUNKS):
+                mx_pass(acc_t[c], codes, ascl, g, wt[(g, c)], "t", g, c, g == 0, g == GROUPS - 1)
 
         for g in range(2):
             t = load_words(wh_words, g, g + 1, 0, H_DIM, "wh%d" % g)
@@ -181,6 +184,7 @@ def tile_ltccell_w_kernel(
         def tau_in(cs):
             for c in cs:
                 nc.vector.tensor_tensor(out=v[c][:], in0=acc_t[c][:], in1=bbc[0][:, cols[c]], op=ALU.add)
+            for c in cs:
                 nc.vector.scalar_tensor_tensor(
                     out=t1[c][:], in0=v[c][:], scalar=-1.0, in1=v[c][:], op0=ALU.mult, op1=ALU.min
                 )
@@ -210,22 +214,19 @@ def tile_ltccell_w_kernel(
         def tau_keep(cs):
             for c in cs:
                 nc.gpsimd.tensor_tensor(out=t1[c][:], in0=hid_sb[:, cols[c]], in1=v[c][:], op=ALU.mult)
+            for c in cs:
                 nc.gpsimd.tensor_tensor(out=t1[c][:], in0=hid_sb[:, cols[c]], in1=t1[c][:], op=ALU.subtract)
 
         rt = v
         keep = t1
         first = (0, 1)
         second = (2, 3)
-        tau_in(first)
-        tau_exp(first)
-        tau_ln(first)
-        tau_sum(first)
-        tau_ln2(first)
-        tau_recip(first)
-        tau_keep(first)
-        tau_in(second)
-        tau_exp(second)
-        tau_ln(second)
+        every = (0, 1, 2, 3)
+        tau_in(every)
+        tau_exp(every)
+        tau_ln(every)
+        tau_sum(every)
+        tau_ln2(every)
 
         acc_r = [psum.tile([P, NT], F32, tag="p%d" % (4 + c), name="acc_r%d" % c) for c in range(CHUNKS)]
         half_passes(acc_r, wr, "r", 0)
@@ -273,18 +274,17 @@ def tile_ltccell_w_kernel(
                 )
 
         r_in(first)
-        tau_sum(second)
-        tau_ln2(second)
         r_tanh(first)
-        tau_recip(second)
+        tau_recip(every)
+        tau_keep(first)
         tau_keep(second)
         r_gate(first)
         r_transpose(first)
         r_in(second)
-        r_copy(first)
-        r_quant(first)
         r_tanh(second)
+        r_copy(first)
         r_gate(second)
+        r_quant(first)
         acc_h = [psum.tile([P, NT], F32, tag="p%d" % c, name="acc_h%d" % c) for c in range(CHUNKS)]
         for c in range(CHUNKS):
             mx_pass(acc_h[c], codes, ascl, 0, wh[(0, c)], "h", 0, c, True, False)
@@ -295,17 +295,27 @@ def tile_ltccell_w_kernel(
             mx_pass(acc_h[c], codes, ascl, 1, wh[(1, c)], "h", 1, c, False, False)
 
         HALF = NT // 2
-        for c in range(CHUNKS):
+        parts = [slice(0, HALF), slice(HALF, NT)]
+        hz = [const.tile([P, NT], F32, name="hz%d" % c) for c in range(CHUNKS)]
+
+        def h_front(c):
             for g in range(2, GROUPS):
                 mx_pass(acc_h[c], gcodes, gscl, g - 2, wh[(g, c)], "h", g, c, False, g == GROUPS - 1)
-            hz = const.tile([P, NT], F32, name="hz%d" % c)
-            parts = [slice(0, HALF), slice(HALF, NT)]
             for i, s in enumerate(parts):
                 lo = NT * c + HALF * i
-                nc.vector.tensor_tensor(out=hz[:, s], in0=acc_h[c][:, s], in1=bbc[2][:, lo : lo + HALF], op=ALU.add)
+                nc.vector.tensor_tensor(out=hz[c][:, s], in0=acc_h[c][:, s], in1=bbc[2][:, lo : lo + HALF], op=ALU.add)
             for s in parts:
-                nc.scalar.activation(out=hz[:, s], in_=hz[:, s], func=ACT.Tanh)
+                nc.scalar.activation(out=hz[c][:, s], in_=hz[c][:, s], func=ACT.Tanh)
+
+        def h_back(c):
             for s in parts:
-                nc.vector.tensor_tensor(out=hz[:, s], in0=hz[:, s], in1=rt[c][:, s], op=ALU.mult)
-                nc.vector.tensor_tensor(out=hz[:, s], in0=hz[:, s], in1=keep[c][:, s], op=ALU.add)
-            nc.sync.dma_start(out=out[:, cols[c]], in_=hz[:])
+                nc.vector.tensor_tensor(out=hz[c][:, s], in0=hz[c][:, s], in1=rt[c][:, s], op=ALU.mult)
+            for s in parts:
+                nc.vector.tensor_tensor(out=hz[c][:, s], in0=hz[c][:, s], in1=keep[c][:, s], op=ALU.add)
+            nc.sync.dma_start(out=out[:, cols[c]], in_=hz[c][:])
+
+        for c in range(CHUNKS):
+            h_front(c)
+            if c > 0:
+                h_back(c - 1)
+        h_back(CHUNKS - 1)

@@ -178,8 +178,10 @@ def tile_ltccell_w_kernel(
                 for g in range(g0, g1):
                     wh[(g, c)] = t[:, g - g0, :]
 
-        v = [const.tile([P, NT], F32, name="v%d" % c) for c in range(CHUNKS)]
-        t1 = [const.tile([P, NT], F32, name="t1_%d" % c) for c in range(CHUNKS)]
+        v_all = const.tile([P, H_DIM], F32, name="v_all")
+        t1_all = const.tile([P, H_DIM], F32, name="t1_all")
+        v = [v_all[:, cols[c]] for c in range(CHUNKS)]
+        t1 = [t1_all[:, cols[c]] for c in range(CHUNKS)]
 
         def tau_in(cs):
             for c in cs:
@@ -211,11 +213,13 @@ def tile_ltccell_w_kernel(
             for c in cs:
                 nc.scalar.activation(out=v[c][:], in_=t1[c][:], func=ACT.Exp, scale=-1.0)
 
-        def tau_keep(cs):
-            for c in cs:
-                nc.gpsimd.tensor_tensor(out=t1[c][:], in0=hid_sb[:, cols[c]], in1=v[c][:], op=ALU.mult)
-            for c in cs:
-                nc.gpsimd.tensor_tensor(out=t1[c][:], in0=hid_sb[:, cols[c]], in1=t1[c][:], op=ALU.subtract)
+        def keep_mul(cs):
+            w = slice(NT * cs[0], NT * (cs[-1] + 1))
+            nc.vector.tensor_tensor(out=t1_all[:, w], in0=hid_sb[:, w], in1=v_all[:, w], op=ALU.mult)
+
+        def keep_sub(cs):
+            w = slice(NT * cs[0], NT * (cs[-1] + 1))
+            nc.vector.tensor_tensor(out=t1_all[:, w], in0=hid_sb[:, w], in1=t1_all[:, w], op=ALU.subtract)
 
         rt = v
         keep = t1
@@ -273,26 +277,29 @@ def tile_ltccell_w_kernel(
                     in_=gg[c][:],
                 )
 
-        r_in(first)
-        r_tanh(first)
-        tau_recip(every)
-        tau_keep(first)
-        tau_keep(second)
-        r_gate(first)
-        r_transpose(first)
-        r_in(second)
-        r_tanh(second)
-        r_copy(first)
-        r_gate(second)
-        r_quant(first)
         acc_h = [psum.tile([P, NT], F32, tag="p%d" % c, name="acc_h%d" % c) for c in range(CHUNKS)]
         for c in range(CHUNKS):
             mx_pass(acc_h[c], codes, ascl, 0, wh[(0, c)], "h", 0, c, True, False)
+        r_in(first)
+        r_tanh(first)
+        r_in(second)
+        r_tanh(second)
+        tau_recip(first)
+        r_gate(first)
+        r_transpose(first)
+        r_gate(second)
+        r_copy(first)
+        keep_mul(first)
+        r_quant(first)
         r_transpose(second)
-        r_copy(second)
-        r_quant(second)
         for c in range(CHUNKS):
             mx_pass(acc_h[c], codes, ascl, 1, wh[(1, c)], "h", 1, c, False, False)
+        r_copy(second)
+        keep_sub(first)
+        r_quant(second)
+        tau_recip(second)
+        keep_mul(second)
+        keep_sub(second)
 
         HALF = NT // 2
         parts = [slice(0, HALF), slice(HALF, NT)]

@@ -30,7 +30,7 @@ def tile_ltccell_w_kernel(
     with ExitStack() as ctx:
         ctx.enter_context(tc.manual_schedule())
         const = ctx.enter_context(tc.tile_pool(name="const", bufs=1))
-        wpool = ctx.enter_context(tc.tile_pool(name="wpool", bufs=13))
+        wpool = ctx.enter_context(tc.tile_pool(name="wpool", bufs=14))
         psum = ctx.enter_context(tc.psum_pool(name="psum", bufs=1))
         cols = [slice(NT * c, NT * (c + 1)) for c in range(CHUNKS)]
 
@@ -157,6 +157,19 @@ def tile_ltccell_w_kernel(
                 stop=stop,
             )
 
+        def h_pass(acc, i, g):
+            lo, wd = blocks[i]
+            a_codes, a_scl, ga = (codes, ascl, g) if g < 2 else (gcodes, gscl, g - 2)
+            nc.tensor.matmul_mx(
+                out=acc[:],
+                lhsT=a_codes[:, P * ga : P * (ga + 1)].bitcast(FP8X4),
+                lhsT_scale=a_scl[:, P * ga : P * (ga + 1)],
+                rhs=whb[(g, i)].bitcast(FP8X4),
+                rhs_scale=planes["h"][4 * (g % 4) : P, g // 4, lo : lo + wd],
+                start=(g == 0),
+                stop=(g == GROUPS - 1),
+            )
+
         def half_passes(acc, table, nm, half):
             for g in range(GROUPS):
                 for c in (2 * half, 2 * half + 1):
@@ -171,12 +184,17 @@ def tile_ltccell_w_kernel(
             t = load_words(wh_words, g, g + 1, 0, H_DIM, "wh%d" % g)
             for c in range(CHUNKS):
                 wh[(g, c)] = t[:, 0, cols[c]]
-        for c in range(CHUNKS):
-            pieces = [(2, 6)] if c < CHUNKS - 1 else [(2, 5), (5, 6)]
+        blocks = [(0, NT), (NT, NT), (2 * NT, NT), (3 * NT, NT // 2), (3 * NT + NT // 2, NT // 2)]
+        last = len(blocks) - 1
+        whb = {}
+        for i, (lo, wd) in enumerate(blocks):
+            for g in range(2):
+                whb[(g, i)] = wh[(g, lo // NT)][:, lo % NT : lo % NT + wd]
+            pieces = [(2, 6)] if i < last else [(2, 5), (5, 6)]
             for g0, g1 in pieces:
-                t = load_words(wh_words, g0, g1, NT * c, NT * (c + 1), "wh_%d_%d" % (c, g0))
+                t = load_words(wh_words, g0, g1, lo, lo + wd, "wh_%d_%d" % (i, g0))
                 for g in range(g0, g1):
-                    wh[(g, c)] = t[:, g - g0, :]
+                    whb[(g, i)] = t[:, g - g0, :]
 
         v_all = const.tile([P, H_DIM], F32, name="v_all")
         t1_all = const.tile([P, H_DIM], F32, name="t1_all")
@@ -277,9 +295,9 @@ def tile_ltccell_w_kernel(
                     in_=gg[c][:],
                 )
 
-        acc_h = [psum.tile([P, NT], F32, tag="p%d" % c, name="acc_h%d" % c) for c in range(CHUNKS)]
-        for c in range(CHUNKS):
-            mx_pass(acc_h[c], codes, ascl, 0, wh[(0, c)], "h", 0, c, True, False)
+        acc_h = [psum.tile([P, blocks[i][1]], F32, tag="p%d" % i, name="acc_h%d" % i) for i in range(last)]
+        for i in range(last):
+            h_pass(acc_h[i], i, 0)
         r_in(first)
         r_tanh(first)
         r_in(second)
@@ -292,8 +310,8 @@ def tile_ltccell_w_kernel(
         keep_mul(first)
         r_quant(first)
         r_transpose(second)
-        for c in range(CHUNKS):
-            mx_pass(acc_h[c], codes, ascl, 1, wh[(1, c)], "h", 1, c, False, False)
+        for i in range(last):
+            h_pass(acc_h[i], i, 1)
         r_copy(second)
         keep_sub(first)
         r_quant(second)
@@ -301,28 +319,38 @@ def tile_ltccell_w_kernel(
         keep_mul(second)
         keep_sub(second)
 
+        acc_h.append(psum.tile([P, blocks[last][1]], F32, tag="p4", name="acc_h%d" % last))
+        h_pass(acc_h[last], last, 0)
+        h_pass(acc_h[last], last, 1)
         HALF = NT // 2
-        parts = [slice(0, HALF), slice(HALF, NT)]
-        hz = [const.tile([P, NT], F32, name="hz%d" % c) for c in range(CHUNKS)]
+        hz = const.tile([P, H_DIM], F32, name="hz")
 
-        def h_front(c):
+        def parts(i):
+            lo, wd = blocks[i]
+            return [(lo + HALF * j, HALF * j) for j in range(wd // HALF)]
+
+        def h_front(i):
             for g in range(2, GROUPS):
-                mx_pass(acc_h[c], gcodes, gscl, g - 2, wh[(g, c)], "h", g, c, False, g == GROUPS - 1)
-            for i, s in enumerate(parts):
-                lo = NT * c + HALF * i
-                nc.vector.tensor_tensor(out=hz[c][:, s], in0=acc_h[c][:, s], in1=bbc[2][:, lo : lo + HALF], op=ALU.add)
-            for s in parts:
-                nc.scalar.activation(out=hz[c][:, s], in_=hz[c][:, s], func=ACT.Tanh)
+                h_pass(acc_h[i], i, g)
+            for lo, off in parts(i):
+                nc.vector.tensor_tensor(
+                    out=hz[:, lo : lo + HALF], in0=acc_h[i][:, off : off + HALF], in1=bbc[2][:, lo : lo + HALF], op=ALU.add
+                )
+            for lo, off in parts(i):
+                nc.scalar.activation(out=hz[:, lo : lo + HALF], in_=hz[:, lo : lo + HALF], func=ACT.Tanh)
 
-        def h_back(c):
-            for s in parts:
-                nc.vector.tensor_tensor(out=hz[c][:, s], in0=hz[c][:, s], in1=rt[c][:, s], op=ALU.mult)
-            for s in parts:
-                nc.vector.tensor_tensor(out=hz[c][:, s], in0=hz[c][:, s], in1=keep[c][:, s], op=ALU.add)
-            nc.sync.dma_start(out=out[:, cols[c]], in_=hz[c][:])
+        def h_back(i, add_engine):
+            for lo, off in parts(i):
+                w = slice(lo, lo + HALF)
+                nc.vector.tensor_tensor(out=hz[:, w], in0=hz[:, w], in1=v_all[:, w], op=ALU.mult)
+            for lo, off in parts(i):
+                w = slice(lo, lo + HALF)
+                add_engine.tensor_tensor(out=hz[:, w], in0=hz[:, w], in1=t1_all[:, w], op=ALU.add)
+            lo, wd = blocks[i]
+            nc.sync.dma_start(out=out[:, lo : lo + wd], in_=hz[:, lo : lo + wd])
 
-        for c in range(CHUNKS):
-            h_front(c)
-            if c > 0:
-                h_back(c - 1)
-        h_back(CHUNKS - 1)
+        for i in range(len(blocks)):
+            h_front(i)
+            if i > 0:
+                h_back(i - 1, nc.gpsimd if i - 1 < 3 else nc.vector)
+        h_back(last, nc.vector)

@@ -30,7 +30,7 @@ def tile_ltccell_w_kernel(
     with ExitStack() as ctx:
         ctx.enter_context(tc.manual_schedule())
         const = ctx.enter_context(tc.tile_pool(name="const", bufs=1))
-        wpool = ctx.enter_context(tc.tile_pool(name="wpool", bufs=14))
+        wpool = ctx.enter_context(tc.tile_pool(name="wpool", bufs=13))
         psum = ctx.enter_context(tc.psum_pool(name="psum", bufs=1))
         cols = [slice(NT * c, NT * (c + 1)) for c in range(CHUNKS)]
 
@@ -93,8 +93,10 @@ def tile_ltccell_w_kernel(
             t = load_words(wt_words, g, g + 1, 0, H_DIM, "wt%d" % g)
             for c in range(CHUNKS):
                 wt[(g, c)] = t[:, 0, cols[c]]
-        for i in range(6):
-            load_half_piece(wr, wr_words, i, "wr")
+        for g in range(GROUPS):
+            t = load_words(wr_words, g, g + 1, 0, H_DIM, "wr%d" % g)
+            for c in range(CHUNKS):
+                wr[(g, c)] = t[:, 0, cols[c]]
 
         codes = const.tile([P, GROUPS * P], U32, align_bytes=64, name="codes")
         ascl = const.tile([P, GROUPS * P], U8, align_bytes=64, name="ascl")
@@ -157,19 +159,6 @@ def tile_ltccell_w_kernel(
                 stop=stop,
             )
 
-        def h_pass(acc, i, g):
-            lo, wd = blocks[i]
-            a_codes, a_scl, ga = (codes, ascl, g) if g < 2 else (gcodes, gscl, g - 2)
-            nc.tensor.matmul_mx(
-                out=acc[:],
-                lhsT=a_codes[:, P * ga : P * (ga + 1)].bitcast(FP8X4),
-                lhsT_scale=a_scl[:, P * ga : P * (ga + 1)],
-                rhs=whb[(g, i)].bitcast(FP8X4),
-                rhs_scale=planes["h"][4 * (g % 4) : P, g // 4, lo : lo + wd],
-                start=(g == 0),
-                stop=(g == GROUPS - 1),
-            )
-
         def half_passes(acc, table, nm, half):
             for g in range(GROUPS):
                 for c in (2 * half, 2 * half + 1):
@@ -184,17 +173,12 @@ def tile_ltccell_w_kernel(
             t = load_words(wh_words, g, g + 1, 0, H_DIM, "wh%d" % g)
             for c in range(CHUNKS):
                 wh[(g, c)] = t[:, 0, cols[c]]
-        blocks = [(0, NT), (NT, NT), (2 * NT, NT), (3 * NT, NT // 2), (3 * NT + NT // 2, NT // 2)]
-        last = len(blocks) - 1
-        whb = {}
-        for i, (lo, wd) in enumerate(blocks):
-            for g in range(2):
-                whb[(g, i)] = wh[(g, lo // NT)][:, lo % NT : lo % NT + wd]
-            pieces = [(2, 6)] if i < last else [(2, 5), (5, 6)]
+        for c in range(CHUNKS):
+            pieces = [(2, 6)] if c < CHUNKS - 1 else [(2, 5), (5, 6)]
             for g0, g1 in pieces:
-                t = load_words(wh_words, g0, g1, lo, lo + wd, "wh_%d_%d" % (i, g0))
+                t = load_words(wh_words, g0, g1, NT * c, NT * (c + 1), "wh_%d_%d" % (c, g0))
                 for g in range(g0, g1):
-                    whb[(g, i)] = t[:, g - g0, :]
+                    wh[(g, c)] = t[:, g - g0, :]
 
         v_all = const.tile([P, H_DIM], F32, name="v_all")
         t1_all = const.tile([P, H_DIM], F32, name="t1_all")
@@ -251,8 +235,9 @@ def tile_ltccell_w_kernel(
         tau_ln2(every)
 
         acc_r = [psum.tile([P, NT], F32, tag="p%d" % (4 + c), name="acc_r%d" % c) for c in range(CHUNKS)]
-        half_passes(acc_r, wr, "r", 0)
-        half_passes(acc_r, wr, "r", 1)
+        for g in range(GROUPS):
+            for c in range(CHUNKS):
+                mx_pass(acc_r[c], codes, ascl, g, wr[(g, c)], "r", g, c, g == 0, g == GROUPS - 1)
 
         vr = [const.tile([P, NT], F32, name="vr%d" % c) for c in range(CHUNKS)]
         gated = [const.tile([P, NT], BF16, name="gated%d" % c) for c in range(CHUNKS)]
@@ -295,9 +280,9 @@ def tile_ltccell_w_kernel(
                     in_=gg[c][:],
                 )
 
-        acc_h = [psum.tile([P, blocks[i][1]], F32, tag="p%d" % i, name="acc_h%d" % i) for i in range(last)]
-        for i in range(last):
-            h_pass(acc_h[i], i, 0)
+        acc_h = [psum.tile([P, NT], F32, tag="p%d" % c, name="acc_h%d" % c) for c in range(CHUNKS)]
+        for c in range(CHUNKS):
+            mx_pass(acc_h[c], codes, ascl, 0, wh[(0, c)], "h", 0, c, True, False)
         r_in(first)
         r_tanh(first)
         r_in(second)
@@ -310,8 +295,8 @@ def tile_ltccell_w_kernel(
         keep_mul(first)
         r_quant(first)
         r_transpose(second)
-        for i in range(last):
-            h_pass(acc_h[i], i, 1)
+        for c in range(CHUNKS):
+            mx_pass(acc_h[c], codes, ascl, 1, wh[(1, c)], "h", 1, c, False, False)
         r_copy(second)
         keep_sub(first)
         r_quant(second)
@@ -319,38 +304,28 @@ def tile_ltccell_w_kernel(
         keep_mul(second)
         keep_sub(second)
 
-        acc_h.append(psum.tile([P, blocks[last][1]], F32, tag="p4", name="acc_h%d" % last))
-        h_pass(acc_h[last], last, 0)
-        h_pass(acc_h[last], last, 1)
         HALF = NT // 2
-        hz = const.tile([P, H_DIM], F32, name="hz")
+        parts = [slice(0, HALF), slice(HALF, NT)]
+        hz = [const.tile([P, NT], F32, name="hz%d" % c) for c in range(CHUNKS)]
 
-        def parts(i):
-            lo, wd = blocks[i]
-            return [(lo + HALF * j, HALF * j) for j in range(wd // HALF)]
-
-        def h_front(i):
+        def h_front(c):
             for g in range(2, GROUPS):
-                h_pass(acc_h[i], i, g)
-            for lo, off in parts(i):
-                nc.vector.tensor_tensor(
-                    out=hz[:, lo : lo + HALF], in0=acc_h[i][:, off : off + HALF], in1=bbc[2][:, lo : lo + HALF], op=ALU.add
-                )
-            for lo, off in parts(i):
-                nc.scalar.activation(out=hz[:, lo : lo + HALF], in_=hz[:, lo : lo + HALF], func=ACT.Tanh)
+                mx_pass(acc_h[c], gcodes, gscl, g - 2, wh[(g, c)], "h", g, c, False, g == GROUPS - 1)
+            for i, s in enumerate(parts):
+                lo = NT * c + HALF * i
+                nc.vector.tensor_tensor(out=hz[c][:, s], in0=acc_h[c][:, s], in1=bbc[2][:, lo : lo + HALF], op=ALU.add)
+            for s in parts:
+                nc.scalar.activation(out=hz[c][:, s], in_=hz[c][:, s], func=ACT.Tanh)
 
-        def h_back(i, add_engine):
-            for lo, off in parts(i):
-                w = slice(lo, lo + HALF)
-                nc.vector.tensor_tensor(out=hz[:, w], in0=hz[:, w], in1=v_all[:, w], op=ALU.mult)
-            for lo, off in parts(i):
-                w = slice(lo, lo + HALF)
-                add_engine.tensor_tensor(out=hz[:, w], in0=hz[:, w], in1=t1_all[:, w], op=ALU.add)
-            lo, wd = blocks[i]
-            nc.sync.dma_start(out=out[:, lo : lo + wd], in_=hz[:, lo : lo + wd])
+        def h_back(c):
+            for s in parts:
+                nc.vector.tensor_tensor(out=hz[c][:, s], in0=hz[c][:, s], in1=rt[c][:, s], op=ALU.mult)
+            for s in parts:
+                nc.vector.tensor_tensor(out=hz[c][:, s], in0=hz[c][:, s], in1=keep[c][:, s], op=ALU.add)
+            nc.sync.dma_start(out=out[:, cols[c]], in_=hz[c][:])
 
-        for i in range(len(blocks)):
-            h_front(i)
-            if i > 0:
-                h_back(i - 1, nc.gpsimd if i - 1 < 3 else nc.vector)
-        h_back(last, nc.vector)
+        for c in range(CHUNKS):
+            h_front(c)
+            if c > 0:
+                h_back(c - 1)
+        h_back(CHUNKS - 1)

@@ -41,14 +41,15 @@ def tile_ltccell_w_kernel(
         one_col = const.tile([P, 1], F32, name="one_col")
         eps_col = const.tile([P, 1], F32, name="eps_col")
         nc.vector.memset(planes["t"][:].bitcast(I32), 0)
-        nc.vector.memset(brow[:].bitcast(I32), 0)
         nc.vector.memset(planes["r"][:].bitcast(I32), 0)
         nc.vector.memset(planes["h"][:].bitcast(I32), 0)
+        nc.vector.memset(brow[:].bitcast(I32), 0)
         nc.vector.memset(one_col[:], 1.0)
         nc.vector.memset(eps_col[:], EPS)
         identf = const.tile([P, P], F32, name="identf")
         identb = const.tile([P, P], BF16, name="identb")
         make_identity(nc, identf[:])
+        make_identity(nc, identb[:])
 
         def load_words(words, g0, g1, n0, n1, name):
             t = wpool.tile([P, g1 - g0, n1 - n0], U32, tag="w", name=name, align_bytes=64)
@@ -56,12 +57,13 @@ def tile_ltccell_w_kernel(
             nc.sync.dma_start(out=t[:].bitcast(I32), in_=src)
             return t
 
-        def load_scales(nm, scales, blk, q):
+        def load_scales(queue, dt, nm, scales, blk):
             ng = 4 if blk == 0 else 2
-            nc.gpsimd.dma_start(
-                out=planes[nm][32 * q : 32 * q + 4 * ng, blk, :].bitcast(F32),
-                in_=scales[4 * blk : 4 * blk + ng, 4 * q : 4 * q + 4, :].bitcast(F32),
-            )
+            for q in range(4):
+                queue.dma_start(
+                    out=planes[nm][32 * q : 32 * q + 4 * ng, blk, :].bitcast(dt),
+                    in_=scales[4 * blk : 4 * blk + ng, 4 * q : 4 * q + 4, :].bitcast(dt),
+                )
 
         def load_half_piece(table, words, i, name):
             half = i // 3
@@ -75,20 +77,15 @@ def tile_ltccell_w_kernel(
         hid_sb = const.tile([P, H_DIM], BF16, name="hid_sb")
         nc.sync.dma_start(out=x_sb[:], in_=x)
         nc.sync.dma_start(out=hid_sb[:], in_=hidden)
+        for nm, scales in (("t", wt_scales), ("r", wr_scales), ("h", wh_scales)):
+            load_scales(nc.sync, I32, nm, scales, 0)
+            load_scales(nc.gpsimd, F32, nm, scales, 1)
         for j, b in enumerate((b_tau, b_r, b_h)):
             nc.scalar.dma_start(out=brow[j : j + 1, :], in_=b.unsqueeze(0))
 
         wt = {}
         wr = {}
         wh = {}
-        later = [(blk, q) for blk in range(2) for q in range(4)]
-        for blk, q in later:
-            load_scales("t", wt_scales, blk, q)
-        make_identity(nc, identb[:])
-        for blk, q in later:
-            load_scales("r", wr_scales, blk, q)
-        for blk, q in later:
-            load_scales("h", wh_scales, blk, q)
         for g in range(GROUPS):
             t = load_words(wt_words, g, g + 1, 0, H_DIM, "wt%d" % g)
             for c in range(CHUNKS):

from contextlib import ExitStack

import concourse.mybir as mybir
from concourse.masks import make_identity

F32 = mybir.dt.float32
BF16 = mybir.dt.bfloat16
I32 = mybir.dt.int32
U32 = mybir.dt.uint32
U8 = mybir.dt.uint8
FP8X4 = mybir.dt.float8_e4m3fn_x4
ALU = mybir.AluOpType
ACT = mybir.ActivationFunctionType

P = 128
I_DIM = 1024
H_DIM = 2048
GROUPS = 6
NT = 512
CHUNKS = H_DIM // NT
EPS = 1e-6

FLOPS = 3 * 2 * 128 * 3072 * 2048


def tile_ltccell_w_kernel(
    tc, x, hidden, wt_words, wt_scales, b_tau, wr_words, wr_scales, b_r, wh_words, wh_scales, b_h, out
):
    nc = tc.nc
    with ExitStack() as ctx:
        ctx.enter_context(tc.manual_schedule())
        const = ctx.enter_context(tc.tile_pool(name="const", bufs=1))
        wpool = ctx.enter_context(tc.tile_pool(name="wpool", bufs=13))
        psum = ctx.enter_context(tc.psum_pool(name="psum", bufs=1))
        cols = [slice(NT * c, NT * (c + 1)) for c in range(CHUNKS)]

        planes = {}
        for nm in ("t", "r", "h"):
            planes[nm] = const.tile([P, 2, H_DIM], U8, align_bytes=64, name="planes_" + nm)
        brow = const.tile([P, H_DIM], BF16, name="brow")
        one_col = const.tile([P, 1], F32, name="one_col")
        eps_col = const.tile([P, 1], F32, name="eps_col")
        nc.vector.memset(planes["t"][:].bitcast(I32), 0)
        nc.vector.memset(planes["r"][:].bitcast(I32), 0)
        nc.vector.memset(planes["h"][:].bitcast(I32), 0)
        nc.vector.memset(brow[:].bitcast(I32), 0)
        nc.vector.memset(one_col[:], 1.0)
        nc.vector.memset(eps_col[:], EPS)
        identf = const.tile([P, P], F32, name="identf")
        identb = const.tile([P, P], BF16, name="identb")
        make_identity(nc, identf[:])
        make_identity(nc, identb[:])

        def load_words(words, g0, g1, n0, n1, name):
            t = wpool.tile([P, g1 - g0, n1 - n0], U32, tag="w", name=name, align_bytes=64)
            src = words[g0:g1, :, n0:n1, :].rearrange("g p n t -> p g (n t)").bitcast(I32)
            nc.sync.dma_start(out=t[:].bitcast(I32), in_=src)
            return t

        def load_scales(queue, dt, nm, scales, blk):
            ng = 4 if blk == 0 else 2
            for q in range(4):
                queue.dma_start(
                    out=planes[nm][32 * q : 32 * q + 4 * ng, blk, :].bitcast(dt),
                    in_=scales[4 * blk : 4 * blk + ng, 4 * q : 4 * q + 4, :].bitcast(dt),
                )

        def load_half_piece(table, words, i, name):
            half = i // 3
            g0 = 2 * (i % 3)
            t = load_words(words, g0, g0 + 2, 2 * NT * half, 2 * NT * (half + 1), "%s%d" % (name, i))
            for g in (g0, g0 + 1):
                for cc in range(2):
                    table[(g, 2 * half + cc)] = t[:, g - g0, NT * cc : NT * (cc + 1)]

        x_sb = const.tile([P, I_DIM], BF16, name="x_sb")
        hid_sb = const.tile([P, H_DIM], BF16, name="hid_sb")
        nc.sync.dma_start(out=x_sb[:], in_=x)
        nc.sync.dma_start(out=hid_sb[:], in_=hidden)
        for nm, scales in (("t", wt_scales), ("r", wr_scales), ("h", wh_scales)):
            load_scales(nc.sync, I32, nm, scales, 0)
            load_scales(nc.gpsimd, F32, nm, scales, 1)
        for j, b in enumerate((b_tau, b_r, b_h)):
            nc.scalar.dma_start(out=brow[j : j + 1, :], in_=b.unsqueeze(0))

        wt = {}
        wr = {}
        wh = {}
        for g in range(GROUPS):
            t = load_words(wt_words, g, g + 1, 0, H_DIM, "wt%d" % g)
            for c in range(CHUNKS):
                wt[(g, c)] = t[:, 0, cols[c]]
        for g in range(GROUPS):
            t = load_words(wr_words, g, g + 1, 0, H_DIM, "wr%d" % g)
            for c in range(CHUNKS):
                wr[(g, c)] = t[:, 0, cols[c]]

        codes = const.tile([P, GROUPS * P], U32, align_bytes=64, name="codes")
        ascl = const.tile([P, GROUPS * P], U8, align_bytes=64, name="ascl")
        xw = x_sb[:].bitcast(F32)
        hw = hid_sb[:].bitcast(F32)
        tps = []
        for j in range(3):
            tp = psum.tile([P, 4, P], F32, tag="p%d" % (4 + j), name="tp%d" % j)
            for gi in range(2):
                g = 2 * j + gi
                srcw = xw if g < 2 else hw
                base = 256 * g if g < 2 else 256 * (g - 2)
                for u in range(2):
                    nc.tensor.transpose(tp[:, 2 * gi + u, :], srcw[:, base + u : base + 256 : 2], identf[:])
            tps.append(tp)
        grouped = [const.tile([P, 2 * NT], BF16, align_bytes=64, name="grp%d" % j) for j in range(3)]
        for j in (0, 1, 2):
            dst = grouped[j][:].bitcast(F32).rearrange("p (g b u) -> p g b u", g=2, u=2)
            src = tps[j][:].rearrange("p (g u) b -> p g b u", g=2)
            if j == 1:
                nc.scalar.copy(out=dst, in_=src)
            else:
                nc.vector.tensor_copy(out=dst, in_=src)
        for j in range(3):
            nc.vector.quantize_mx(
                out=codes[:, 256 * j : 256 * (j + 1)].bitcast(FP8X4),
                scales=ascl[:, 256 * j : 256 * (j + 1)],
                in_=grouped[j][:],
            )
        hh = const.tile([P, H_DIM], BF16, name="hh")
        nc.vector.tensor_scalar_mul(out=hh[:], in0=hid_sb[:], scalar1=0.5)

        bbc = []
        tags = [7, 4, 5, 6, 7, 4]
        for j in range(3):
            bb = const.tile([P, H_DIM], BF16, name="bbc%d" % j)
            for half in range(2):
                pb = psum.tile([P, 2 * NT], BF16, tag="p%d" % tags[2 * j + half], name="pb%d_%d" % (j, half))
                for s in range(2):
                    lo = 2 * NT * half + NT * s
                    nc.tensor.matmul(
                        out=pb[:, NT * s : NT * (s + 1)],
                        lhsT=identb[:, j : j + 1].to_broadcast([P, P]),
                        rhs=brow[:, lo : lo + NT],
                        start=True,
                        stop=True,
                    )
                nc.scalar.copy(out=bb[:, 2 * NT * half : 2 * NT * (half + 1)], in_=pb[:])
            bbc.append(bb)

        def mx_pass(acc, a_codes, a_scl, ga, w_ap, nm, g, c, start, stop):
            k = 4 * (g % 4)
            nc.tensor.matmul_mx(
                out=acc[:],
                lhsT=a_codes[:, P * ga : P * (ga + 1)].bitcast(FP8X4),
                lhsT_scale=a_scl[:, P * ga : P * (ga + 1)],
                rhs=w_ap.bitcast(FP8X4),
                rhs_scale=planes[nm][k:P, g // 4, NT * c : NT * (c + 1)],
                start=start,
                stop=stop,
            )

        def half_passes(acc, table, nm, half):
            for g in range(GROUPS):
                for c in (2 * half, 2 * half + 1):
                    mx_pass(acc[c], codes, ascl, g, table[(g, c)], nm, g, c, g == 0, g == GROUPS - 1)

        acc_t = [psum.tile([P, NT], F32, tag="p%d" % c, name="acc_t%d" % c) for c in range(CHUNKS)]
        for g in range(GROUPS):
            for c in range(CHUNKS):
                mx_pass(acc_t[c], codes, ascl, g, wt[(g, c)], "t", g, c, g == 0, g == GROUPS - 1)

        for g in range(2):
            t = load_words(wh_words, g, g + 1, 0, H_DIM, "wh%d" % g)
            for c in range(CHUNKS):
                wh[(g, c)] = t[:, 0, cols[c]]
        for c in range(CHUNKS):
            pieces = [(2, 6)] if c < CHUNKS - 1 else [(2, 5), (5, 6)]
            for g0, g1 in pieces:
                t = load_words(wh_words, g0, g1, NT * c, NT * (c + 1), "wh_%d_%d" % (c, g0))
                for g in range(g0, g1):
                    wh[(g, c)] = t[:, g - g0, :]

        v_all = const.tile([P, H_DIM], F32, name="v_all")
        t1_all = const.tile([P, H_DIM], F32, name="t1_all")
        v = [v_all[:, cols[c]] for c in range(CHUNKS)]
        t1 = [t1_all[:, cols[c]] for c in range(CHUNKS)]

        def tau_in(cs):
            for c in cs:
                nc.vector.tensor_tensor(out=v[c][:], in0=acc_t[c][:], in1=bbc[0][:, cols[c]], op=ALU.add)
            for c in cs:
                nc.vector.scalar_tensor_tensor(
                    out=t1[c][:], in0=v[c][:], scalar=-1.0, in1=v[c][:], op0=ALU.mult, op1=ALU.min
                )

        def tau_exp(cs):
            for c in cs:
                nc.scalar.activation(out=t1[c][:], in_=t1[c][:], func=ACT.Exp)

        def tau_ln(cs):
            for c in cs:
                nc.scalar.activation(out=t1[c][:], in_=t1[c][:], func=ACT.Ln, bias=one_col[:])

        def tau_sum(cs):
            for c in cs:
                nc.vector.scalar_tensor_tensor(
                    out=v[c][:], in0=v[c][:], scalar=0.0, in1=t1[c][:], op0=ALU.max, op1=ALU.add
                )

        def tau_ln2(cs):
            for c in cs:
                nc.scalar.activation(out=t1[c][:], in_=v[c][:], func=ACT.Ln, bias=eps_col[:])

        def tau_recip(cs):
            for c in cs:
                nc.scalar.activation(out=v[c][:], in_=t1[c][:], func=ACT.Exp, scale=-1.0)

        def keep_mul(cs):
            w = slice(NT * cs[0], NT * (cs[-1] + 1))
            nc.vector.tensor_tensor(out=t1_all[:, w], in0=hid_sb[:, w], in1=v_all[:, w], op=ALU.mult)

        def keep_sub(cs):
            w = slice(NT * cs[0], NT * (cs[-1] + 1))
            nc.vector.tensor_tensor(out=t1_all[:, w], in0=hid_sb[:, w], in1=t1_all[:, w], op=ALU.subtract)

        rt = v
        keep = t1
        first = (0, 1)
        second = (2, 3)
        every = (0, 1, 2, 3)
        tau_in(every)
        tau_exp(every)
        tau_ln(every)
        tau_sum(every)
        tau_ln2(every)

        acc_r = [psum.tile([P, NT], F32, tag="p%d" % (4 + c), name="acc_r%d" % c) for c in range(CHUNKS)]
        for g in range(GROUPS):
            for c in range(CHUNKS):
                mx_pass(acc_r[c], codes, ascl, g, wr[(g, c)], "r", g, c, g == 0, g == GROUPS - 1)

        vr = [const.tile([P, NT], F32, name="vr%d" % c) for c in range(CHUNKS)]
        gated = [const.tile([P, NT], BF16, name="gated%d" % c) for c in range(CHUNKS)]
        gg = [const.tile([P, NT], BF16, align_bytes=64, name="gg%d" % c) for c in range(CHUNKS)]
        gcodes = const.tile([P, CHUNKS * P], U32, align_bytes=64, name="gcodes")
        gscl = const.tile([P, CHUNKS * P], U8, align_bytes=64, name="gscl")
        tpg = {}

        def r_in(cs):
            for c in cs:
                nc.vector.tensor_tensor(out=vr[c][:], in0=acc_r[c][:], in1=bbc[1][:, cols[c]], op=ALU.add)

        def r_tanh(cs):
            for c in cs:
                nc.scalar.activation(out=vr[c][:], in_=vr[c][:], func=ACT.Tanh, scale=0.5)

        def r_gate(cs):
            for c in cs:
                nc.vector.scalar_tensor_tensor(
                    out=gated[c][:], in0=vr[c][:], scalar=1.0, in1=hh[:, cols[c]], op0=ALU.add, op1=ALU.mult
                )

        def r_transpose(cs):
            for c in cs:
                tpg[c] = psum.tile([P, 4, P], BF16, tag="p%d" % (4 + c), name="tpg%d" % c)
                for t in range(4):
                    nc.tensor.transpose(tpg[c][:, t, :], gated[c][:, t:NT:4], identb[:])

        def r_copy(cs):
            for c in cs:
                nc.scalar.copy(
                    out=gg[c][:].rearrange("p (b t) -> p b t", t=4), in_=tpg[c][:].rearrange("p t b -> p b t")
                )

        def r_quant(cs):
            for c in cs:
                nc.vector.quantize_mx(
                    out=gcodes[:, P * c : P * (c + 1)].bitcast(FP8X4),
                    scales=gscl[:, P * c : P * (c + 1)],
                    in_=gg[c][:],
                )

        acc_h = [psum.tile([P, NT], F32, tag="p%d" % c, name="acc_h%d" % c) for c in range(CHUNKS)]
        for c in range(CHUNKS):
            mx_pass(acc_h[c], codes, ascl, 0, wh[(0, c)], "h", 0, c, True, False)
        r_in(first)
        r_tanh(first)
        r_in(second)
        r_tanh(second)
        tau_recip(first)
        r_gate(first)
        r_transpose(first)
        r_gate(second)
        r_copy(first)
        keep_mul(first)
        r_quant(first)
        r_transpose(second)
        for c in range(CHUNKS):
            mx_pass(acc_h[c], codes, ascl, 1, wh[(1, c)], "h", 1, c, False, False)
        r_copy(second)
        keep_sub(first)
        r_quant(second)
        tau_recip(second)
        keep_mul(second)
        keep_sub(second)

        HALF = NT // 2
        parts = [slice(0, HALF), slice(HALF, NT)]
        hz = [const.tile([P, NT], F32, name="hz%d" % c) for c in range(CHUNKS)]

        def h_front(c):
            for g in range(2, GROUPS):
                mx_pass(acc_h[c], gcodes, gscl, g - 2, wh[(g, c)], "h", g, c, False, g == GROUPS - 1)
            for i, s in enumerate(parts):
                lo = NT * c + HALF * i
                nc.vector.tensor_tensor(out=hz[c][:, s], in0=acc_h[c][:, s], in1=bbc[2][:, lo : lo + HALF], op=ALU.add)
            for s in parts:
                nc.scalar.activation(out=hz[c][:, s], in_=hz[c][:, s], func=ACT.Tanh)

        def h_back(c):
            for s in parts:
                nc.vector.tensor_tensor(out=hz[c][:, s], in0=hz[c][:, s], in1=rt[c][:, s], op=ALU.mult)
            for s in parts:
                nc.vector.tensor_tensor(out=hz[c][:, s], in0=hz[c][:, s], in1=keep[c][:, s], op=ALU.add)
            nc.sync.dma_start(out=out[:, cols[c]], in_=hz[c][:])

        for c in range(CHUNKS):
            h_front(c)
            if c > 0:
                h_back(c - 1)
        h_back(CHUNKS - 1)
